import numpy as np
import ml_dtypes

BF16 = ml_dtypes.bfloat16


def bf(x):
    return np.asarray(x, np.float32).astype(BF16)


def f32(x):
    return np.asarray(x, np.float32)


def f64(x):
    return np.asarray(x).astype(np.float64)


def striped(idx):
    return np.tile(idx.reshape(-1, 16).T, (8, 1))


D, S, M, N = 128, 2048, 512, 1024
POS_DIV = 3.0


def setup_inputs():
    return {"table": bf(np.random.standard_normal((D, S))), "pos": bf(np.random.standard_normal((D, N))), "w": bf(np.random.standard_normal((D, M)) / np.sqrt(D)), "offs": striped(np.random.permutation(np.tile(np.arange(S), 2))[:N])}


def reference(table, pos, w, offs):
    idx = offs[:16].T.reshape(-1)
    return f64(w).T @ f64(table)[:, idx] + (f64(w).T @ f64(pos)) / POS_DIV

@@ -1,0 +1,67 @@
+import concourse.mybir as mybir
+
+BF16, F32, U16 = mybir.dt.bfloat16, mybir.dt.float32, mybir.dt.uint16
+
+P = 128
+WORDS = 2048
+ROWS = 512
+TOKENS = 1024
+PIECE = 512
+BLOCKS = ROWS // P
+PIECES = TOKENS // PIECE
+LIST_COLUMNS = PIECE // 16
+BANKS = 8
+
+FLOPS = 2 * 2 * P * ROWS * TOKENS
+
+
+def tile_lstransformer_kernel(tc, table, pos, w, offs, out):
+    nc = tc.nc
+    with (
+        tc.tile_pool(name="held", bufs=1) as held,
+        tc.tile_pool(name="results", bufs=4) as results,
+        tc.psum_pool(name="banks", bufs=BANKS) as banks,
+    ):
+        offsets = held.tile([P, TOKENS // 16], U16, name="offsets")
+        words = held.tile([P, WORDS], BF16, name="words")
+        weights = held.tile([P, ROWS], BF16, name="weights")
+        places = held.tile([P, TOKENS], BF16, name="places")
+        nc.sync.dma_start(offsets[:], offs)
+        nc.scalar.dma_start(weights[:], w)
+        nc.scalar.dma_start(places[:], pos)
+        nc.sync.dma_start(words[:], table)
+
+        thirds = held.tile([P, BLOCKS * TOKENS], F32, name="thirds")
+        for block in range(BLOCKS):
+            for piece in range(PIECES):
+                pos_bank = banks.tile([P, PIECE], F32, name="pos_bank", tag="bank")
+                nc.tensor.matmul(
+                    pos_bank[:],
+                    weights[:, block * P : (block + 1) * P],
+                    places[:, piece * PIECE : (piece + 1) * PIECE],
+                    start=True,
+                    stop=True,
+                )
+                at = block * TOKENS + piece * PIECE
+                nc.scalar.activation(
+                    thirds[:, at : at + PIECE], pos_bank[:], mybir.ActivationFunctionType.Copy, scale=1.0 / 3.0
+                )
+
+        for block in range(BLOCKS):
+            for piece in range(PIECES):
+                word_bank = banks.tile([P, PIECE], F32, name="word_bank", tag="bank")
+                nc.tensor.matmul(
+                    word_bank[:],
+                    weights[:, block * P : (block + 1) * P],
+                    words[:].indirect(offsets[:, piece * LIST_COLUMNS : (piece + 1) * LIST_COLUMNS]),
+                    start=True,
+                    stop=True,
+                )
+                at = block * TOKENS + piece * PIECE
+                result = results.tile([P, PIECE], F32, name="result")
+                nc.vector.tensor_tensor(
+                    result[:], word_bank[:], thirds[:, at : at + PIECE], mybir.AluOpType.add
+                )
+                nc.sync.dma_start(
+                    out[block * P : (block + 1) * P, piece * PIECE : (piece + 1) * PIECE], result[:]
+                )

@@ -19,7 +19,7 @@ def tile_lstransformer_kernel(tc, table, pos, w, offs, out):
     nc = tc.nc
     with (
         tc.tile_pool(name="held", bufs=1) as held,
-        tc.tile_pool(name="results", bufs=4) as results,
+        tc.tile_pool(name="results", bufs=BLOCKS * PIECES) as results,
         tc.psum_pool(name="banks", bufs=BANKS) as banks,
     ):
         offsets = held.tile([P, TOKENS // 16], U16, name="offsets")

@@ -27,13 +27,16 @@ def tile_lstransformer_kernel(tc, table, pos, w, offs, out):
         weights = held.tile([P, ROWS], BF16, name="weights")
         places = held.tile([P, TOKENS], BF16, name="places")
         nc.sync.dma_start(offsets[:], offs)
-        nc.scalar.dma_start(weights[:], w)
-        nc.scalar.dma_start(places[:], pos)
+        nc.sync.dma_start(weights[:], w)
+        for piece in range(PIECES):
+            nc.sync.dma_start(
+                places[:, piece * PIECE : (piece + 1) * PIECE], pos[:, piece * PIECE : (piece + 1) * PIECE]
+            )
         nc.sync.dma_start(words[:], table)
 
         thirds = held.tile([P, BLOCKS * TOKENS], F32, name="thirds")
-        for block in range(BLOCKS):
-            for piece in range(PIECES):
+        for piece in range(PIECES):
+            for block in range(BLOCKS):
                 pos_bank = banks.tile([P, PIECE], F32, name="pos_bank", tag="bank")
                 nc.tensor.matmul(
                     pos_bank[:],
@@ -47,8 +50,8 @@ def tile_lstransformer_kernel(tc, table, pos, w, offs, out):
                     thirds[:, at : at + PIECE], pos_bank[:], mybir.ActivationFunctionType.Copy, scale=1.0 / 3.0
                 )
 
-        for block in range(BLOCKS):
-            for piece in range(PIECES):
+        for piece in range(PIECES):
+            for block in range(BLOCKS):
                 word_bank = banks.tile([P, PIECE], F32, name="word_bank", tag="bank")
                 nc.tensor.matmul(
                     word_bank[:],

@@ -11,6 +11,7 @@ BLOCKS = ROWS // P
 PIECES = TOKENS // PIECE
 LIST_COLUMNS = PIECE // 16
 BANKS = 8
+WARM_UPS = 6
 
 FLOPS = 2 * 2 * P * ROWS * TOKENS
 
@@ -33,6 +34,12 @@ def tile_lstransformer_kernel(tc, table, pos, w, offs, out):
                 places[:, piece * PIECE : (piece + 1) * PIECE], pos[:, piece * PIECE : (piece + 1) * PIECE]
             )
         nc.sync.dma_start(words[:], table)
+
+        zeros = held.tile([P, PIECE], BF16, name="zeros")
+        nc.vector.memset(zeros[:], 0.0)
+        warm_bank = banks.tile([P, PIECE], F32, name="warm_bank", tag="bank")
+        for turn in range(WARM_UPS):
+            nc.tensor.matmul(warm_bank[:], zeros[:, :P], zeros[:], start=True, stop=True)
 
         thirds = held.tile([P, BLOCKS * TOKENS], F32, name="thirds")
         for piece in range(PIECES):

@@ -11,7 +11,7 @@ BLOCKS = ROWS // P
 PIECES = TOKENS // PIECE
 LIST_COLUMNS = PIECE // 16
 BANKS = 8
-WARM_UPS = 6
+WARM_UPS = 3
 
 FLOPS = 2 * 2 * P * ROWS * TOKENS
 

@@ -72,6 +72,7 @@ def tile_lstransformer_kernel(tc, table, pos, w, offs, out):
                 nc.vector.tensor_tensor(
                     result[:], word_bank[:], thirds[:, at : at + PIECE], mybir.AluOpType.add
                 )
-                nc.sync.dma_start(
+                store_queue = nc.sync if block % 2 == 0 else nc.scalar
+                store_queue.dma_start(
                     out[block * P : (block + 1) * P, piece * PIECE : (piece + 1) * PIECE], result[:]
                 )

@@ -21,6 +21,7 @@ def tile_lstransformer_kernel(tc, table, pos, w, offs, out):
     with (
         tc.tile_pool(name="held", bufs=1) as held,
         tc.tile_pool(name="results", bufs=BLOCKS * PIECES) as results,
+        tc.tile_pool(name="copies", bufs=PIECES) as copies,
         tc.psum_pool(name="banks", bufs=BANKS) as banks,
     ):
         offsets = held.tile([P, TOKENS // 16], U16, name="offsets")
@@ -69,10 +70,16 @@ def tile_lstransformer_kernel(tc, table, pos, w, offs, out):
                 )
                 at = block * TOKENS + piece * PIECE
                 result = results.tile([P, PIECE], F32, name="result")
-                nc.vector.tensor_tensor(
-                    result[:], word_bank[:], thirds[:, at : at + PIECE], mybir.AluOpType.add
-                )
-                store_queue = nc.sync if block % 2 == 0 else nc.scalar
-                store_queue.dma_start(
+                if block == 0:
+                    copied = copies.tile([P, PIECE], F32, name="copied")
+                    nc.scalar.copy(copied[:], word_bank[:])
+                    nc.gpsimd.tensor_tensor(
+                        result[:], copied[:], thirds[:, at : at + PIECE], mybir.AluOpType.add
+                    )
+                else:
+                    nc.vector.tensor_tensor(
+                        result[:], word_bank[:], thirds[:, at : at + PIECE], mybir.AluOpType.add
+                    )
+                nc.sync.dma_start(
                     out[block * P : (block + 1) * P, piece * PIECE : (piece + 1) * PIECE], result[:]
                 )

@@ -21,19 +21,17 @@ def tile_lstransformer_kernel(tc, table, pos, w, offs, out):
     with (
         tc.tile_pool(name="held", bufs=1) as held,
         tc.tile_pool(name="results", bufs=BLOCKS * PIECES) as results,
-        tc.tile_pool(name="copies", bufs=PIECES) as copies,
         tc.psum_pool(name="banks", bufs=BANKS) as banks,
     ):
         offsets = held.tile([P, TOKENS // 16], U16, name="offsets")
         words = held.tile([P, WORDS], BF16, name="words")
         weights = held.tile([P, ROWS], BF16, name="weights")
         places = held.tile([P, TOKENS], BF16, name="places")
+        nc.sync.dma_start(weights[:, :P], w[:, :P])
+        nc.sync.dma_start(places[:, :PIECE], pos[:, :PIECE])
+        nc.sync.dma_start(weights[:, P:], w[:, P:])
+        nc.sync.dma_start(places[:, PIECE:], pos[:, PIECE:])
         nc.sync.dma_start(offsets[:], offs)
-        nc.sync.dma_start(weights[:], w)
-        for piece in range(PIECES):
-            nc.sync.dma_start(
-                places[:, piece * PIECE : (piece + 1) * PIECE], pos[:, piece * PIECE : (piece + 1) * PIECE]
-            )
         nc.sync.dma_start(words[:], table)
 
         zeros = held.tile([P, PIECE], BF16, name="zeros")
@@ -70,16 +68,9 @@ def tile_lstransformer_kernel(tc, table, pos, w, offs, out):
                 )
                 at = block * TOKENS + piece * PIECE
                 result = results.tile([P, PIECE], F32, name="result")
-                if block == 0:
-                    copied = copies.tile([P, PIECE], F32, name="copied")
-                    nc.scalar.copy(copied[:], word_bank[:])
-                    nc.gpsimd.tensor_tensor(
-                        result[:], copied[:], thirds[:, at : at + PIECE], mybir.AluOpType.add
-                    )
-                else:
-                    nc.vector.tensor_tensor(
-                        result[:], word_bank[:], thirds[:, at : at + PIECE], mybir.AluOpType.add
-                    )
+                nc.vector.tensor_tensor(
+                    result[:], word_bank[:], thirds[:, at : at + PIECE], mybir.AluOpType.add
+                )
                 nc.sync.dma_start(
                     out[block * P : (block + 1) * P, piece * PIECE : (piece + 1) * PIECE], result[:]
                 )

@@ -20,7 +20,7 @@ def tile_lstransformer_kernel(tc, table, pos, w, offs, out):
     nc = tc.nc
     with (
         tc.tile_pool(name="held", bufs=1) as held,
-        tc.tile_pool(name="results", bufs=BLOCKS * PIECES) as results,
+        tc.tile_pool(name="results", bufs=BLOCKS * PIECES + 2) as results,
         tc.psum_pool(name="banks", bufs=BANKS) as banks,
     ):
         offsets = held.tile([P, TOKENS // 16], U16, name="offsets")
@@ -56,21 +56,21 @@ def tile_lstransformer_kernel(tc, table, pos, w, offs, out):
                     thirds[:, at : at + PIECE], pos_bank[:], mybir.ActivationFunctionType.Copy, scale=1.0 / 3.0
                 )
 
-        for piece in range(PIECES):
-            for block in range(BLOCKS):
-                word_bank = banks.tile([P, PIECE], F32, name="word_bank", tag="bank")
-                nc.tensor.matmul(
-                    word_bank[:],
-                    weights[:, block * P : (block + 1) * P],
-                    words[:].indirect(offsets[:, piece * LIST_COLUMNS : (piece + 1) * LIST_COLUMNS]),
-                    start=True,
-                    stop=True,
-                )
-                at = block * TOKENS + piece * PIECE
-                result = results.tile([P, PIECE], F32, name="result")
-                nc.vector.tensor_tensor(
-                    result[:], word_bank[:], thirds[:, at : at + PIECE], mybir.AluOpType.add
-                )
-                nc.sync.dma_start(
-                    out[block * P : (block + 1) * P, piece * PIECE : (piece + 1) * PIECE], result[:]
-                )
+        products = [(block, piece * PIECE, PIECE) for piece in range(PIECES) for block in range(BLOCKS)]
+        last_block, last_first, last_tokens = products[-1]
+        products = products[:-1] + [
+            (last_block, last_first + start, tokens) for start, tokens in ((0, PIECE // 2), (PIECE // 2, PIECE // 4), (3 * PIECE // 4, PIECE // 4))
+        ]
+        for block, first, tokens in products:
+            word_bank = banks.tile([P, tokens], F32, name="word_bank", tag="bank")
+            nc.tensor.matmul(
+                word_bank[:],
+                weights[:, block * P : (block + 1) * P],
+                words[:].indirect(offsets[:, first // 16 : (first + tokens) // 16]),
+                start=True,
+                stop=True,
+            )
+            at = block * TOKENS + first
+            result = results.tile([P, tokens], F32, name="result")
+            nc.vector.tensor_tensor(result[:], word_bank[:], thirds[:, at : at + tokens], mybir.AluOpType.add)
+            nc.sync.dma_start(out[block * P : (block + 1) * P, first : first + tokens], result[:])

@@ -52,15 +52,16 @@ def tile_lstransformer_kernel(tc, table, pos, w, offs, out):
                     stop=True,
                 )
                 at = block * TOKENS + piece * PIECE
-                nc.scalar.activation(
-                    thirds[:, at : at + PIECE], pos_bank[:], mybir.ActivationFunctionType.Copy, scale=1.0 / 3.0
-                )
+                if piece == 0 and block % 2 == 1:
+                    nc.vector.tensor_scalar_mul(thirds[:, at : at + PIECE], pos_bank[:], 1.0 / 3.0)
+                else:
+                    nc.scalar.activation(
+                        thirds[:, at : at + PIECE], pos_bank[:], mybir.ActivationFunctionType.Copy, scale=1.0 / 3.0
+                    )
 
         products = [(block, piece * PIECE, PIECE) for piece in range(PIECES) for block in range(BLOCKS)]
-        last_block, last_first, last_tokens = products[-1]
-        products = products[:-1] + [
-            (last_block, last_first + start, tokens) for start, tokens in ((0, PIECE // 2), (PIECE // 2, PIECE // 4), (3 * PIECE // 4, PIECE // 4))
-        ]
+        first_block, first_first, first_tokens = products[0]
+        products = [(first_block, first_first + start, tokens) for start, tokens in ((0, PIECE // 4), (PIECE // 4, PIECE // 4), (PIECE // 2, PIECE // 2))] + products[1:]
         for block, first, tokens in products:
             word_bank = banks.tile([P, tokens], F32, name="word_bank", tag="bank")
             nc.tensor.matmul(

@@ -7,11 +7,12 @@ WORDS = 2048
 ROWS = 512
 TOKENS = 1024
 PIECE = 512
+HALF = PIECE // 2
 BLOCKS = ROWS // P
 PIECES = TOKENS // PIECE
 LIST_COLUMNS = PIECE // 16
 BANKS = 8
-WARM_UPS = 3
+WARM_UPS = 12
 
 FLOPS = 2 * 2 * P * ROWS * TOKENS
 
@@ -20,7 +21,7 @@ def tile_lstransformer_kernel(tc, table, pos, w, offs, out):
     nc = tc.nc
     with (
         tc.tile_pool(name="held", bufs=1) as held,
-        tc.tile_pool(name="results", bufs=BLOCKS * PIECES + 2) as results,
+        tc.tile_pool(name="results", bufs=BLOCKS * PIECES + 1) as results,
         tc.psum_pool(name="banks", bufs=BANKS) as banks,
     ):
         offsets = held.tile([P, TOKENS // 16], U16, name="offsets")
@@ -28,29 +29,32 @@ def tile_lstransformer_kernel(tc, table, pos, w, offs, out):
         weights = held.tile([P, ROWS], BF16, name="weights")
         places = held.tile([P, TOKENS], BF16, name="places")
         nc.sync.dma_start(weights[:, :P], w[:, :P])
-        nc.sync.dma_start(places[:, :PIECE], pos[:, :PIECE])
+        nc.scalar.dma_start(places[:, :HALF], pos[:, :HALF])
+        nc.sync.dma_start(places[:, HALF:PIECE], pos[:, HALF:PIECE])
         nc.sync.dma_start(weights[:, P:], w[:, P:])
         nc.sync.dma_start(places[:, PIECE:], pos[:, PIECE:])
         nc.sync.dma_start(offsets[:], offs)
         nc.sync.dma_start(words[:], table)
 
-        zeros = held.tile([P, PIECE], BF16, name="zeros")
+        zeros = held.tile([P, P], BF16, name="zeros")
         nc.vector.memset(zeros[:], 0.0)
         warm_bank = banks.tile([P, PIECE], F32, name="warm_bank", tag="bank")
         for turn in range(WARM_UPS):
-            nc.tensor.matmul(warm_bank[:], zeros[:, :P], zeros[:], start=True, stop=True)
+            nc.tensor.matmul(warm_bank[:, :P], zeros[:], zeros[:], start=True, stop=True)
 
         thirds = held.tile([P, BLOCKS * TOKENS], F32, name="thirds")
         for piece in range(PIECES):
             for block in range(BLOCKS):
                 pos_bank = banks.tile([P, PIECE], F32, name="pos_bank", tag="bank")
-                nc.tensor.matmul(
-                    pos_bank[:],
-                    weights[:, block * P : (block + 1) * P],
-                    places[:, piece * PIECE : (piece + 1) * PIECE],
-                    start=True,
-                    stop=True,
-                )
+                widths = (HALF, HALF) if piece == 0 and block == 0 else (PIECE,)
+                for part, width in enumerate(widths):
+                    nc.tensor.matmul(
+                        pos_bank[:, part * width : (part + 1) * width],
+                        weights[:, block * P : (block + 1) * P],
+                        places[:, piece * PIECE + part * width : piece * PIECE + (part + 1) * width],
+                        start=True,
+                        stop=True,
+                    )
                 at = block * TOKENS + piece * PIECE
                 if piece == 0 and block % 2 == 1:
                     nc.vector.tensor_scalar_mul(thirds[:, at : at + PIECE], pos_bank[:], 1.0 / 3.0)
@@ -61,7 +65,7 @@ def tile_lstransformer_kernel(tc, table, pos, w, offs, out):
 
         products = [(block, piece * PIECE, PIECE) for piece in range(PIECES) for block in range(BLOCKS)]
         first_block, first_first, first_tokens = products[0]
-        products = [(first_block, first_first + start, tokens) for start, tokens in ((0, PIECE // 4), (PIECE // 4, PIECE // 4), (PIECE // 2, PIECE // 2))] + products[1:]
+        products = [(first_block, first_first + start, tokens) for start, tokens in ((0, PIECE // 4), (PIECE // 4, 3 * PIECE // 4))] + products[1:]
         for block, first, tokens in products:
             word_bank = banks.tile([P, tokens], F32, name="word_bank", tag="bank")
             nc.tensor.matmul(

@@ -29,7 +29,7 @@ def tile_lstransformer_kernel(tc, table, pos, w, offs, out):
         weights = held.tile([P, ROWS], BF16, name="weights")
         places = held.tile([P, TOKENS], BF16, name="places")
         nc.sync.dma_start(weights[:, :P], w[:, :P])
-        nc.scalar.dma_start(places[:, :HALF], pos[:, :HALF])
+        nc.sync.dma_start(places[:, :HALF], pos[:, :HALF])
         nc.sync.dma_start(places[:, HALF:PIECE], pos[:, HALF:PIECE])
         nc.sync.dma_start(weights[:, P:], w[:, P:])
         nc.sync.dma_start(places[:, PIECE:], pos[:, PIECE:])

@@ -63,19 +63,29 @@ def tile_lstransformer_kernel(tc, table, pos, w, offs, out):
                         thirds[:, at : at + PIECE], pos_bank[:], mybir.ActivationFunctionType.Copy, scale=1.0 / 3.0
                     )
 
-        products = [(block, piece * PIECE, PIECE) for piece in range(PIECES) for block in range(BLOCKS)]
-        first_block, first_first, first_tokens = products[0]
-        products = [(first_block, first_first + start, tokens) for start, tokens in ((0, PIECE // 4), (PIECE // 4, 3 * PIECE // 4))] + products[1:]
-        for block, first, tokens in products:
-            word_bank = banks.tile([P, tokens], F32, name="word_bank", tag="bank")
-            nc.tensor.matmul(
-                word_bank[:],
-                weights[:, block * P : (block + 1) * P],
-                words[:].indirect(offsets[:, first // 16 : (first + tokens) // 16]),
-                start=True,
-                stop=True,
-            )
-            at = block * TOKENS + first
-            result = results.tile([P, tokens], F32, name="result")
-            nc.vector.tensor_tensor(result[:], word_bank[:], thirds[:, at : at + tokens], mybir.AluOpType.add)
-            nc.sync.dma_start(out[block * P : (block + 1) * P, first : first + tokens], result[:])
+        for piece in range(PIECES):
+            for block in range(BLOCKS):
+                rows = slice(block * P, (block + 1) * P)
+                at = block * TOKENS + piece * PIECE
+                result = results.tile([P, PIECE], F32, name="result")
+                last = piece == PIECES - 1 and block == BLOCKS - 1
+                for start in range(0, PIECE, HALF):
+                    first = piece * PIECE + start
+                    word_bank = banks.tile([P, HALF], F32, name="word_bank", tag="bank")
+                    nc.tensor.matmul(
+                        word_bank[:],
+                        weights[:, rows],
+                        words[:].indirect(offsets[:, first // 16 : (first + HALF) // 16]),
+                        start=True,
+                        stop=True,
+                    )
+                    nc.vector.tensor_tensor(
+                        result[:, start : start + HALF],
+                        word_bank[:],
+                        thirds[:, at + start : at + start + HALF],
+                        mybir.AluOpType.add,
+                    )
+                    if last:
+                        nc.sync.dma_start(out[rows, first : first + HALF], result[:, start : start + HALF])
+                if not last:
+                    nc.sync.dma_start(out[rows, piece * PIECE : (piece + 1) * PIECE], result[:])

@@ -11,6 +11,7 @@ HALF = PIECE // 2
 BLOCKS = ROWS // P
 PIECES = TOKENS // PIECE
 LIST_COLUMNS = PIECE // 16
+EARLY = 7
 BANKS = 8
 WARM_UPS = 12
 
@@ -42,50 +43,84 @@ def tile_lstransformer_kernel(tc, table, pos, w, offs, out):
         for turn in range(WARM_UPS):
             nc.tensor.matmul(warm_bank[:, :P], zeros[:], zeros[:], start=True, stop=True)
 
-        thirds = held.tile([P, BLOCKS * TOKENS], F32, name="thirds")
-        for piece in range(PIECES):
-            for block in range(BLOCKS):
-                pos_bank = banks.tile([P, PIECE], F32, name="pos_bank", tag="bank")
-                widths = (HALF, HALF) if piece == 0 and block == 0 else (PIECE,)
-                for part, width in enumerate(widths):
-                    nc.tensor.matmul(
-                        pos_bank[:, part * width : (part + 1) * width],
-                        weights[:, block * P : (block + 1) * P],
-                        places[:, piece * PIECE + part * width : piece * PIECE + (part + 1) * width],
-                        start=True,
-                        stop=True,
-                    )
-                at = block * TOKENS + piece * PIECE
-                if piece == 0 and block % 2 == 1:
-                    nc.vector.tensor_scalar_mul(thirds[:, at : at + PIECE], pos_bank[:], 1.0 / 3.0)
-                else:
-                    nc.scalar.activation(
-                        thirds[:, at : at + PIECE], pos_bank[:], mybir.ActivationFunctionType.Copy, scale=1.0 / 3.0
-                    )
+        products = [(block, piece) for piece in range(PIECES) for block in range(BLOCKS)]
+        early, late = products[:EARLY], products[EARLY:]
 
-        for piece in range(PIECES):
-            for block in range(BLOCKS):
-                rows = slice(block * P, (block + 1) * P)
-                at = block * TOKENS + piece * PIECE
+        thirds = held.tile([P, BLOCKS * TOKENS], F32, name="thirds")
+        for block, piece in early:
+            pos_bank = banks.tile([P, PIECE], F32, name="pos_bank", tag="bank")
+            width = HALF if (block, piece) == products[0] else PIECE
+            for start in range(0, PIECE, width):
+                nc.tensor.matmul(
+                    pos_bank[:, start : start + width],
+                    weights[:, block * P : (block + 1) * P],
+                    places[:, piece * PIECE + start : piece * PIECE + start + width],
+                    start=True,
+                    stop=True,
+                )
+            at = block * TOKENS + piece * PIECE
+            if piece == 0 and block % 2 == 1:
+                nc.vector.tensor_scalar_mul(thirds[:, at : at + PIECE], pos_bank[:], 1.0 / 3.0)
+            else:
+                nc.scalar.activation(
+                    thirds[:, at : at + PIECE], pos_bank[:], mybir.ActivationFunctionType.Copy, scale=1.0 / 3.0
+                )
+
+        word_banks = []
+        kept_of = {}
+        for block, piece in products:
+            rows = slice(block * P, (block + 1) * P)
+            at = block * TOKENS + piece * PIECE
+            is_early = (block, piece) in early
+            if is_early:
                 result = results.tile([P, PIECE], F32, name="result")
-                last = piece == PIECES - 1 and block == BLOCKS - 1
-                for start in range(0, PIECE, HALF):
-                    first = piece * PIECE + start
-                    word_bank = banks.tile([P, HALF], F32, name="word_bank", tag="bank")
-                    nc.tensor.matmul(
-                        word_bank[:],
-                        weights[:, rows],
-                        words[:].indirect(offsets[:, first // 16 : (first + HALF) // 16]),
-                        start=True,
-                        stop=True,
-                    )
+            else:
+                kept = results.tile([P, PIECE], F32, name="kept")
+                kept_of[block, piece] = kept
+            for start in range(0, PIECE, HALF):
+                first = piece * PIECE + start
+                word_bank = banks.tile([P, HALF], F32, name="word_bank", tag="bank")
+                word_banks.append(word_bank)
+                nc.tensor.matmul(
+                    word_bank[:],
+                    weights[:, rows],
+                    words[:].indirect(offsets[:, first // 16 : (first + HALF) // 16]),
+                    start=True,
+                    stop=True,
+                )
+                if is_early:
                     nc.vector.tensor_tensor(
                         result[:, start : start + HALF],
                         word_bank[:],
                         thirds[:, at + start : at + start + HALF],
                         mybir.AluOpType.add,
                     )
-                    if last:
-                        nc.sync.dma_start(out[rows, first : first + HALF], result[:, start : start + HALF])
-                if not last:
-                    nc.sync.dma_start(out[rows, piece * PIECE : (piece + 1) * PIECE], result[:])
+                else:
+                    nc.scalar.activation(
+                        kept[:, start : start + HALF], word_bank[:], mybir.ActivationFunctionType.Copy
+                    )
+            if is_early:
+                nc.sync.dma_start(out[rows, piece * PIECE : (piece + 1) * PIECE], result[:])
+
+        late_halves = [(block, piece, start) for block, piece in late for start in range(0, PIECE, HALF)]
+        freed = word_banks[2 * EARLY - len(late_halves) : 2 * EARLY]
+        for (block, piece, start), pos_half in zip(late_halves, freed):
+            rows = slice(block * P, (block + 1) * P)
+            first = piece * PIECE + start
+            if start == 0:
+                late_result = results.tile([P, PIECE], F32, name="late_result")
+            nc.tensor.matmul(
+                pos_half[:], weights[:, rows], places[:, first : first + HALF], start=True, stop=True
+            )
+            nc.vector.scalar_tensor_tensor(
+                late_result[:, start : start + HALF],
+                pos_half[:],
+                1.0 / 3.0,
+                kept_of[block, piece][:, start : start + HALF],
+                mybir.AluOpType.mult,
+                mybir.AluOpType.add,
+            )
+            if (block, piece) == products[-1]:
+                nc.sync.dma_start(out[rows, first : first + HALF], late_result[:, start : start + HALF])
+            elif start == HALF:
+                nc.sync.dma_start(out[rows, piece * PIECE : (piece + 1) * PIECE], late_result[:])

@@ -12,6 +12,7 @@ BLOCKS = ROWS // P
 PIECES = TOKENS // PIECE
 LIST_COLUMNS = PIECE // 16
 EARLY = 7
+IN_HALVES = 2
 BANKS = 8
 WARM_UPS = 12
 
@@ -66,7 +67,7 @@ def tile_lstransformer_kernel(tc, table, pos, w, offs, out):
                     thirds[:, at : at + PIECE], pos_bank[:], mybir.ActivationFunctionType.Copy, scale=1.0 / 3.0
                 )
 
-        word_banks = []
+        early_banks = []
         kept_of = {}
         for block, piece in products:
             rows = slice(block * P, (block + 1) * P)
@@ -77,44 +78,45 @@ def tile_lstransformer_kernel(tc, table, pos, w, offs, out):
             else:
                 kept = results.tile([P, PIECE], F32, name="kept")
                 kept_of[block, piece] = kept
-            for start in range(0, PIECE, HALF):
+            width = PIECE if (block, piece) in products[IN_HALVES:EARLY] else HALF
+            for start in range(0, PIECE, width):
                 first = piece * PIECE + start
-                word_bank = banks.tile([P, HALF], F32, name="word_bank", tag="bank")
-                word_banks.append(word_bank)
+                word_bank = banks.tile([P, width], F32, name="word_bank", tag="bank")
                 nc.tensor.matmul(
                     word_bank[:],
                     weights[:, rows],
-                    words[:].indirect(offsets[:, first // 16 : (first + HALF) // 16]),
+                    words[:].indirect(offsets[:, first // 16 : (first + width) // 16]),
                     start=True,
                     stop=True,
                 )
                 if is_early:
+                    early_banks.append(word_bank)
                     nc.vector.tensor_tensor(
-                        result[:, start : start + HALF],
+                        result[:, start : start + width],
                         word_bank[:],
-                        thirds[:, at + start : at + start + HALF],
+                        thirds[:, at + start : at + start + width],
                         mybir.AluOpType.add,
                     )
                 else:
                     nc.scalar.activation(
-                        kept[:, start : start + HALF], word_bank[:], mybir.ActivationFunctionType.Copy
+                        kept[:, start : start + width], word_bank[:], mybir.ActivationFunctionType.Copy
                     )
             if is_early:
                 nc.sync.dma_start(out[rows, piece * PIECE : (piece + 1) * PIECE], result[:])
 
         late_halves = [(block, piece, start) for block, piece in late for start in range(0, PIECE, HALF)]
-        freed = word_banks[2 * EARLY - len(late_halves) : 2 * EARLY]
+        freed = early_banks[-1 - len(late_halves) : -1]
         for (block, piece, start), pos_half in zip(late_halves, freed):
             rows = slice(block * P, (block + 1) * P)
             first = piece * PIECE + start
             if start == 0:
                 late_result = results.tile([P, PIECE], F32, name="late_result")
             nc.tensor.matmul(
-                pos_half[:], weights[:, rows], places[:, first : first + HALF], start=True, stop=True
+                pos_half[:, :HALF], weights[:, rows], places[:, first : first + HALF], start=True, stop=True
             )
             nc.vector.scalar_tensor_tensor(
                 late_result[:, start : start + HALF],
-                pos_half[:],
+                pos_half[:, :HALF],
                 1.0 / 3.0,
                 kept_of[block, piece][:, start : start + HALF],
                 mybir.AluOpType.mult,

@@ -14,7 +14,7 @@ LIST_COLUMNS = PIECE // 16
 EARLY = 7
 IN_HALVES = 2
 BANKS = 8
-WARM_UPS = 12
+WARM_UPS = 3
 
 FLOPS = 2 * 2 * P * ROWS * TOKENS
 
@@ -42,7 +42,13 @@ def tile_lstransformer_kernel(tc, table, pos, w, offs, out):
         nc.vector.memset(zeros[:], 0.0)
         warm_bank = banks.tile([P, PIECE], F32, name="warm_bank", tag="bank")
         for turn in range(WARM_UPS):
-            nc.tensor.matmul(warm_bank[:, :P], zeros[:], zeros[:], start=True, stop=True)
+            nc.tensor.matmul(
+                warm_bank[:].rearrange("p (a b) -> p a b", b=P),
+                zeros[:],
+                zeros[:].unsqueeze(1).to_broadcast([P, PIECE // P, P]),
+                start=True,
+                stop=True,
+            )
 
         products = [(block, piece) for piece in range(PIECES) for block in range(BLOCKS)]
         early, late = products[:EARLY], products[EARLY:]

import concourse.mybir as mybir

BF16, F32, U16 = mybir.dt.bfloat16, mybir.dt.float32, mybir.dt.uint16

P = 128
WORDS = 2048
ROWS = 512
TOKENS = 1024
PIECE = 512
HALF = PIECE // 2
BLOCKS = ROWS // P
PIECES = TOKENS // PIECE
LIST_COLUMNS = PIECE // 16
EARLY = 7
IN_HALVES = 2
BANKS = 8
WARM_UPS = 3

FLOPS = 2 * 2 * P * ROWS * TOKENS


def tile_lstransformer_kernel(tc, table, pos, w, offs, out):
    nc = tc.nc
    with (
        tc.tile_pool(name="held", bufs=1) as held,
        tc.tile_pool(name="results", bufs=BLOCKS * PIECES + 1) as results,
        tc.psum_pool(name="banks", bufs=BANKS) as banks,
    ):
        offsets = held.tile([P, TOKENS // 16], U16, name="offsets")
        words = held.tile([P, WORDS], BF16, name="words")
        weights = held.tile([P, ROWS], BF16, name="weights")
        places = held.tile([P, TOKENS], BF16, name="places")
        nc.sync.dma_start(weights[:, :P], w[:, :P])
        nc.sync.dma_start(places[:, :HALF], pos[:, :HALF])
        nc.sync.dma_start(places[:, HALF:PIECE], pos[:, HALF:PIECE])
        nc.sync.dma_start(weights[:, P:], w[:, P:])
        nc.sync.dma_start(places[:, PIECE:], pos[:, PIECE:])
        nc.sync.dma_start(offsets[:], offs)
        nc.sync.dma_start(words[:], table)

        zeros = held.tile([P, P], BF16, name="zeros")
        nc.vector.memset(zeros[:], 0.0)
        warm_bank = banks.tile([P, PIECE], F32, name="warm_bank", tag="bank")
        for turn in range(WARM_UPS):
            nc.tensor.matmul(
                warm_bank[:].rearrange("p (a b) -> p a b", b=P),
                zeros[:],
                zeros[:].unsqueeze(1).to_broadcast([P, PIECE // P, P]),
                start=True,
                stop=True,
            )

        products = [(block, piece) for piece in range(PIECES) for block in range(BLOCKS)]
        early, late = products[:EARLY], products[EARLY:]

        thirds = held.tile([P, BLOCKS * TOKENS], F32, name="thirds")
        for block, piece in early:
            pos_bank = banks.tile([P, PIECE], F32, name="pos_bank", tag="bank")
            width = HALF if (block, piece) == products[0] else PIECE
            for start in range(0, PIECE, width):
                nc.tensor.matmul(
                    pos_bank[:, start : start + width],
                    weights[:, block * P : (block + 1) * P],
                    places[:, piece * PIECE + start : piece * PIECE + start + width],
                    start=True,
                    stop=True,
                )
            at = block * TOKENS + piece * PIECE
            if piece == 0 and block % 2 == 1:
                nc.vector.tensor_scalar_mul(thirds[:, at : at + PIECE], pos_bank[:], 1.0 / 3.0)
            else:
                nc.scalar.activation(
                    thirds[:, at : at + PIECE], pos_bank[:], mybir.ActivationFunctionType.Copy, scale=1.0 / 3.0
                )

        early_banks = []
        kept_of = {}
        for block, piece in products:
            rows = slice(block * P, (block + 1) * P)
            at = block * TOKENS + piece * PIECE
            is_early = (block, piece) in early
            if is_early:
                result = results.tile([P, PIECE], F32, name="result")
            else:
                kept = results.tile([P, PIECE], F32, name="kept")
                kept_of[block, piece] = kept
            width = PIECE if (block, piece) in products[IN_HALVES:EARLY] else HALF
            for start in range(0, PIECE, width):
                first = piece * PIECE + start
                word_bank = banks.tile([P, width], F32, name="word_bank", tag="bank")
                nc.tensor.matmul(
                    word_bank[:],
                    weights[:, rows],
                    words[:].indirect(offsets[:, first // 16 : (first + width) // 16]),
                    start=True,
                    stop=True,
                )
                if is_early:
                    early_banks.append(word_bank)
                    nc.vector.tensor_tensor(
                        result[:, start : start + width],
                        word_bank[:],
                        thirds[:, at + start : at + start + width],
                        mybir.AluOpType.add,
                    )
                else:
                    nc.scalar.activation(
                        kept[:, start : start + width], word_bank[:], mybir.ActivationFunctionType.Copy
                    )
            if is_early:
                nc.sync.dma_start(out[rows, piece * PIECE : (piece + 1) * PIECE], result[:])

        late_halves = [(block, piece, start) for block, piece in late for start in range(0, PIECE, HALF)]
        freed = early_banks[-1 - len(late_halves) : -1]
        for (block, piece, start), pos_half in zip(late_halves, freed):
            rows = slice(block * P, (block + 1) * P)
            first = piece * PIECE + start
            if start == 0:
                late_result = results.tile([P, PIECE], F32, name="late_result")
            nc.tensor.matmul(
                pos_half[:, :HALF], weights[:, rows], places[:, first : first + HALF], start=True, stop=True
            )
            nc.vector.scalar_tensor_tensor(
                late_result[:, start : start + HALF],
                pos_half[:, :HALF],
                1.0 / 3.0,
                kept_of[block, piece][:, start : start + HALF],
                mybir.AluOpType.mult,
                mybir.AluOpType.add,
            )
            if (block, piece) == products[-1]:
                nc.sync.dma_start(out[rows, first : first + HALF], late_result[:, start : start + HALF])
            elif start == HALF:
                nc.sync.dma_start(out[rows, piece * PIECE : (piece + 1) * PIECE], late_result[:])
